import numpy as np
import ml_dtypes


def mxq(x, axis, fmt="e4m3"):
    dtype, down = {"e4m3": (ml_dtypes.float8_e4m3fn, 7), "e5m2": (ml_dtypes.float8_e5m2, 14)}[fmt]
    v = np.moveaxis(np.asarray(x, np.float32).astype(ml_dtypes.bfloat16).astype(np.float64), axis, -1)
    blocks = v.reshape(v.shape[:-1] + (-1, 32))
    amax = np.abs(blocks).max(-1, keepdims=True)
    byte = np.maximum(np.where(amax > 0, np.frexp(amax)[1] - 1 + 127, 0) - down, 1)
    scale = np.exp2(byte - 127.0)
    codes = (blocks / scale).astype(np.float32).astype(dtype).astype(np.float64)
    return np.moveaxis((codes * scale).reshape(v.shape), -1, axis)


WIDE = False


def mx_kscale(k):
    if not WIDE:
        return np.ones(k)
    levels = np.array([10, -10, 5, -5, 0])
    a = np.random.permutation(np.resize(levels, k // 512 * 4)).reshape(k // 512, 4)
    idx = np.arange(k)
    return np.exp2(a[idx // 512, idx % 128 // 32])


BF16 = ml_dtypes.bfloat16


def bf(x):
    return np.asarray(x, np.float32).astype(BF16)


def f64(x):
    return np.asarray(x).astype(np.float64)


B, T, H, KV, D = 1, 512, 16, 4, 128
G = H // KV
NEG = -1e9


def setup_inputs():
    s = mx_kscale(T)
    keep = np.random.random((1, 1, T, T)) < 0.5
    mask_w = np.where(keep, 1.0 + 0.3 * np.random.standard_normal((1, 1, T, T)), 0.0)
    mask_b = np.where(keep, 0.5 * np.random.standard_normal((1, 1, T, T)) + np.log(s)[None, None, None, :], NEG)
    return {"q_rot": bf(np.random.standard_normal((B, T, H, D))),
            "k_rot": bf(np.random.standard_normal((B, T, KV, D))),
            "v": bf(np.random.standard_normal((B, T, KV, D)) * 2.0 * (s.max() / s)[None, :, None, None]),
            "mask_w": bf(mask_w), "mask_b": bf(mask_b)}


def reference(q_rot, k_rot, v, mask_w, mask_b):
    qg = f64(q_rot).transpose(0, 2, 1, 3).reshape(B, KV, G * T, D)
    kt = f64(k_rot).transpose(0, 2, 3, 1)
    s = (qg @ kt).reshape(B, H, T, T) * (1.0 / np.sqrt(D))
    s = s * f64(mask_w) + f64(mask_b)
    e = np.exp(s - s.max(-1, keepdims=True))
    eq = mxq(e.reshape(B, KV, G * T, T), 3, "e4m3")
    vq = mxq(f64(v).transpose(0, 2, 1, 3), 2, "e4m3")
    o = (eq @ vq).reshape(B, H, T, D) / e.sum(-1, keepdims=True)
    return o.transpose(0, 2, 1, 3)

@@ -1,0 +1,217 @@
+from contextlib import ExitStack
+import math
+
+import concourse.mybir as mybir
+from concourse.masks import make_identity
+
+BF16 = mybir.dt.bfloat16
+F32 = mybir.dt.float32
+U32 = mybir.dt.uint32
+U8 = mybir.dt.uint8
+FP8X4 = mybir.dt.float8_e4m3fn_x4
+ALU = mybir.AluOpType
+ACT = mybir.ActivationFunctionType
+AXIS = mybir.AxisListType
+
+P = 128
+T = 512
+H = 16
+KV = 4
+D = 128
+G = H // KV
+QT = T // P
+PACK = 4
+HALF = T // 2
+NG = QT * KV
+SCALE = 1.0 / math.sqrt(D)
+
+FLOPS = 2 * 2 * H * T * T * D
+
+
+def tile_mistralselfattention_pb_kernel(tc, q_rot, k_rot, v, mask_w, mask_b, out):
+    nc = tc.nc
+
+    q_view = q_rot.rearrange("b (qt p) h d -> p (b qt) h d", p=P)
+    k_view = k_rot.rearrange("b (kt p) kv d -> p (b kt) kv d", p=P)
+    mw_view = mask_w.rearrange("a b (qt p) k -> p (a b qt) k", p=P)
+    mb_view = mask_b.rearrange("a b (qt p) k -> p (a b qt) k", p=P)
+    out_view = out.rearrange("b (qt p) h d -> p (b qt) h d", p=P)
+    v_view = v.rearrange("b (u p e) kv d -> p (b u) (e kv d)", u=2, p=P, e=2)
+
+    with ExitStack() as ctx:
+        keep = ctx.enter_context(tc.tile_pool(name="keep", bufs=1))
+        work = ctx.enter_context(tc.tile_pool(name="work", bufs=3))
+        ps_scores = ctx.enter_context(tc.psum_pool(name="ps_scores", bufs=G))
+        ps_e = ctx.enter_context(tc.psum_pool(name="ps_e", bufs=2))
+        ps_qk = ctx.enter_context(tc.psum_pool(name="ps_qk", bufs=1))
+        ps_out = ctx.enter_context(tc.psum_pool(name="ps_out", bufs=1))
+        ctx.enter_context(tc.manual_schedule())
+
+        k_sb = keep.tile([P, QT, KV, D], BF16)
+        v_sb = keep.tile([P, 2, 2 * KV * D], BF16)
+        q_sb = [keep.tile([P, H, D], BF16, name="q_sb%d" % qt) for qt in range(QT)]
+        mw_sb = [keep.tile([P, T], BF16, name="mw_sb%d" % qt) for qt in range(QT)]
+        mb_sb = [keep.tile([P, T], BF16, name="mb_sb%d" % qt) for qt in range(QT)]
+        nc.sync.dma_start(out=k_sb[:], in_=k_view)
+        for qt in range(QT):
+            nc.sync.dma_start(out=q_sb[qt][:], in_=q_view[:, qt])
+            nc.sync.dma_start(out=mw_sb[qt][:], in_=mw_view[:, qt])
+            nc.sync.dma_start(out=mb_sb[qt][:], in_=mb_view[:, qt])
+            if qt == 0:
+                nc.sync.dma_start(out=v_sb[:], in_=v_view)
+
+        ident_bf = keep.tile([P, P], BF16)
+        make_identity(nc, ident_bf[:])
+        ident_f32 = keep.tile([P, P], F32)
+        make_identity(nc, ident_f32[:])
+        warm = keep.tile([P, 1], F32)
+        nc.vector.memset(warm[:], 0.0)
+        nc.scalar.activation(out=warm[:], in_=warm[:], func=ACT.Exp)
+
+        kT = keep.tile([P, KV, T], BF16)
+        v_grouped = keep.tile([P, KV * D, PACK], BF16, align_bytes=64)
+        v_codes = keep.tile([P, KV * D], U32, align_bytes=64)
+        v_scales = keep.tile([P, KV * D], U8, align_bytes=64)
+
+        tiles = {}
+
+        def turn_queries(g):
+            qt, kv = divmod(g, KV)
+            turned = ps_qk.tile([P, 2, G, P], BF16)
+            for i in range(G):
+                nc.tensor.transpose(turned[:, 0, i, :], q_sb[qt][:, kv * G + i, :], ident_bf[:])
+            if qt == 0:
+                for kt in range(QT):
+                    nc.tensor.transpose(turned[:, 1, kt, :], k_sb[:, kt, kv, :], ident_bf[:])
+                nc.scalar.copy(out=kT[:, kv, :], in_=turned[:, 1].rearrange("d kt p -> d (kt p)"))
+            qT = work.tile([P, G, P], BF16)
+            nc.scalar.copy(out=qT[:], in_=turned[:, 0])
+            tiles["qT", g] = qT
+
+        def scores_matmul(g):
+            kv = g % KV
+            for i in range(G):
+                s_ps = ps_scores.tile([P, T], F32)
+                nc.tensor.matmul(
+                    s_ps[:], lhsT=tiles["qT", g][:, i, :], rhs=kT[:, kv, :], start=True, stop=True
+                )
+                tiles["s_ps", g, i] = s_ps
+
+        def weigh_scores(g):
+            qt = g // KV
+            s2 = work.tile([P, G, T], F32)
+            for i in range(G):
+                nc.vector.scalar_tensor_tensor(
+                    out=s2[:, i, :], in0=tiles["s_ps", g, i][:], scalar=SCALE, in1=mw_sb[qt][:],
+                    op0=ALU.mult, op1=ALU.mult,
+                )
+            nc.gpsimd.tensor_tensor(
+                out=s2[:], in0=s2[:],
+                in1=mb_sb[qt][:].unsqueeze(1).to_broadcast([P, G, T]),
+                op=ALU.add,
+            )
+            tiles["s2", g] = s2
+
+        def row_maxima(g):
+            neg_max = work.tile([P, G], F32)
+            nc.vector.tensor_reduce(
+                out=neg_max[:], in_=tiles["s2", g][:], axis=AXIS.X, op=ALU.max, negate=True
+            )
+            tiles["neg_max", g] = neg_max
+
+        def exponentials(g):
+            e_sb = work.tile([P, G, T], BF16)
+            rowsum = work.tile([P, G], F32, bufs=4)
+            for i in range(G):
+                nc.scalar.activation(
+                    out=e_sb[:, i, :], in_=tiles["s2", g][:, i, :], func=ACT.Exp,
+                    bias=tiles["neg_max", g][:, i : i + 1], scale=1.0,
+                    accum_out=rowsum[:, i : i + 1],
+                )
+            tiles["e_sb", g] = e_sb
+            tiles["rowsum", g] = rowsum
+
+        def turn_e(g):
+            for pair in range(G // 2):
+                eT_ps = ps_e.tile([P, 2, 2, P], F32)
+                for j in range(2):
+                    e_words = tiles["e_sb", g][:, 2 * pair + j, :].bitcast(F32)
+                    for u in range(2):
+                        nc.tensor.transpose(
+                            eT_ps[:, j, u, :], e_words[:, u * P : (u + 1) * P], ident_f32[:]
+                        )
+                tiles["eT_ps", g, pair] = eT_ps
+
+        def group_e(g):
+            e_grouped = work.tile([P, G, P, PACK], BF16, align_bytes=64)
+            for pair in range(G // 2):
+                nc.scalar.copy(
+                    out=e_grouped[:, 2 * pair : 2 * pair + 2].bitcast(F32),
+                    in_=tiles["eT_ps", g, pair][:].rearrange("p j u q -> p j q u"),
+                )
+            tiles["e_grouped", g] = e_grouped
+
+        def quantise_e(g):
+            recip = work.tile([P, G], F32)
+            nc.vector.reciprocal(out=recip[:], in_=tiles["rowsum", g][:])
+            tiles["recip", g] = recip
+            if g == 0:
+                nc.vector.quantize_mx(
+                    out=v_codes[:].bitcast(FP8X4),
+                    scales=v_scales[:],
+                    in_=v_grouped[:].rearrange("p c t -> p (c t)"),
+                )
+            e_codes = work.tile([P, G * P], U32, align_bytes=64)
+            e_scales = work.tile([P, G * P], U8, align_bytes=64)
+            nc.vector.quantize_mx(
+                out=e_codes[:].bitcast(FP8X4),
+                scales=e_scales[:],
+                in_=tiles["e_grouped", g][:].rearrange("p i q t -> p (i q t)"),
+            )
+            tiles["e_codes", g] = e_codes
+            tiles["e_scales", g] = e_scales
+
+        def values_matmul(g):
+            kv = g % KV
+            o_ps = ps_out.tile([P, G, D], F32)
+            for i in range(G):
+                nc.tensor.matmul_mx(
+                    out=o_ps[:, i, :],
+                    lhsT=tiles["e_codes", g][:, i * P : (i + 1) * P].bitcast(FP8X4),
+                    lhsT_scale=tiles["e_scales", g][:, i * P : (i + 1) * P],
+                    rhs=v_codes[:, kv * D : (kv + 1) * D].bitcast(FP8X4),
+                    rhs_scale=v_scales[:, kv * D : (kv + 1) * D],
+                    start=True,
+                    stop=True,
+                )
+            tiles["o_ps", g] = o_ps
+
+        def normalise_and_store(g):
+            qt, kv = divmod(g, KV)
+            o_sb = work.tile([P, G, D], F32)
+            for i in range(G):
+                nc.scalar.activation(
+                    out=o_sb[:, i, :], in_=tiles["o_ps", g][:, i, :], func=ACT.Copy,
+                    scale=tiles["recip", g][:, i : i + 1],
+                )
+            nc.sync.dma_start(out=out_view[:, qt, kv * G : (kv + 1) * G, :], in_=o_sb[:])
+
+        def run(stage, g):
+            if 0 <= g < NG:
+                stage(g)
+
+        for k in range(-3, NG + 3):
+            run(quantise_e, k - 2)
+            run(group_e, k - 1)
+            run(scores_matmul, k + 2)
+            run(values_matmul, k - 2)
+            run(normalise_and_store, k - 2)
+            run(turn_queries, k + 3)
+            if k == -1:
+                nc.scalar.copy(
+                    out=v_grouped[:], in_=v_sb[:].rearrange("p u (e c) -> p c (u e)", e=2)
+                )
+            run(row_maxima, k)
+            run(exponentials, k)
+            run(turn_e, k)
+            run(weigh_scores, k + 2)

@@ -121,15 +121,16 @@ def tile_mistralselfattention_pb_kernel(tc, q_rot, k_rot, v, mask_w, mask_b, out
 
         def exponentials(g):
             e_sb = work.tile([P, G, T], BF16)
-            rowsum = work.tile([P, G], F32, bufs=4)
+            if g % 2 == 0:
+                tiles["rowsum", g // 2] = work.tile([P, 2, G], F32, name="rowsum")
+            rowsum = tiles["rowsum", g // 2]
             for i in range(G):
                 nc.scalar.activation(
                     out=e_sb[:, i, :], in_=tiles["s2", g][:, i, :], func=ACT.Exp,
                     bias=tiles["neg_max", g][:, i : i + 1], scale=1.0,
-                    accum_out=rowsum[:, i : i + 1],
+                    accum_out=rowsum[:, g % 2, i : i + 1],
                 )
             tiles["e_sb", g] = e_sb
-            tiles["rowsum", g] = rowsum
 
         def turn_e(g):
             for pair in range(G // 2):
@@ -143,33 +144,36 @@ def tile_mistralselfattention_pb_kernel(tc, q_rot, k_rot, v, mask_w, mask_b, out
                 tiles["eT_ps", g, pair] = eT_ps
 
         def group_e(g):
-            e_grouped = work.tile([P, G, P, PACK], BF16, align_bytes=64)
+            if g % 2 == 0:
+                tiles["e_grouped", g // 2] = work.tile(
+                    [P, 2, G, P, PACK], BF16, name="e_grouped", align_bytes=64
+                )
+            e_grouped = tiles["e_grouped", g // 2]
             for pair in range(G // 2):
                 nc.scalar.copy(
-                    out=e_grouped[:, 2 * pair : 2 * pair + 2].bitcast(F32),
+                    out=e_grouped[:, g % 2, 2 * pair : 2 * pair + 2].bitcast(F32),
                     in_=tiles["eT_ps", g, pair][:].rearrange("p j u q -> p j q u"),
                 )
-            tiles["e_grouped", g] = e_grouped
 
-        def quantise_e(g):
-            recip = work.tile([P, G], F32)
-            nc.vector.reciprocal(out=recip[:], in_=tiles["rowsum", g][:])
-            tiles["recip", g] = recip
-            if g == 0:
+        def quantise_e(two):
+            recip = work.tile([P, 2, G], F32)
+            nc.vector.reciprocal(out=recip[:], in_=tiles["rowsum", two][:])
+            tiles["recip", two] = recip
+            if two == 0:
                 nc.vector.quantize_mx(
                     out=v_codes[:].bitcast(FP8X4),
                     scales=v_scales[:],
                     in_=v_grouped[:].rearrange("p c t -> p (c t)"),
                 )
-            e_codes = work.tile([P, G * P], U32, align_bytes=64)
-            e_scales = work.tile([P, G * P], U8, align_bytes=64)
+            e_codes = work.tile([P, 2, G, P], U32, align_bytes=64)
+            e_scales = work.tile([P, 2, G, P], U8, align_bytes=64)
             nc.vector.quantize_mx(
-                out=e_codes[:].bitcast(FP8X4),
-                scales=e_scales[:],
-                in_=tiles["e_grouped", g][:].rearrange("p i q t -> p (i q t)"),
+                out=e_codes[:].rearrange("p a i q -> p (a i q)").bitcast(FP8X4),
+                scales=e_scales[:].rearrange("p a i q -> p (a i q)"),
+                in_=tiles["e_grouped", two][:].rearrange("p a i q t -> p (a i q t)"),
             )
-            tiles["e_codes", g] = e_codes
-            tiles["e_scales", g] = e_scales
+            tiles["e_codes", two] = e_codes
+            tiles["e_scales", two] = e_scales
 
         def values_matmul(g):
             kv = g % KV
@@ -177,8 +181,8 @@ def tile_mistralselfattention_pb_kernel(tc, q_rot, k_rot, v, mask_w, mask_b, out
             for i in range(G):
                 nc.tensor.matmul_mx(
                     out=o_ps[:, i, :],
-                    lhsT=tiles["e_codes", g][:, i * P : (i + 1) * P].bitcast(FP8X4),
-                    lhsT_scale=tiles["e_scales", g][:, i * P : (i + 1) * P],
+                    lhsT=tiles["e_codes", g // 2][:, g % 2, i, :].bitcast(FP8X4),
+                    lhsT_scale=tiles["e_scales", g // 2][:, g % 2, i, :],
                     rhs=v_codes[:, kv * D : (kv + 1) * D].bitcast(FP8X4),
                     rhs_scale=v_scales[:, kv * D : (kv + 1) * D],
                     start=True,
@@ -192,7 +196,7 @@ def tile_mistralselfattention_pb_kernel(tc, q_rot, k_rot, v, mask_w, mask_b, out
             for i in range(G):
                 nc.scalar.activation(
                     out=o_sb[:, i, :], in_=tiles["o_ps", g][:, i, :], func=ACT.Copy,
-                    scale=tiles["recip", g][:, i : i + 1],
+                    scale=tiles["recip", g // 2][:, g % 2, i : i + 1],
                 )
             nc.sync.dma_start(out=out_view[:, qt, kv * G : (kv + 1) * G, :], in_=o_sb[:])
 
@@ -201,11 +205,12 @@ def tile_mistralselfattention_pb_kernel(tc, q_rot, k_rot, v, mask_w, mask_b, out
                 stage(g)
 
         for k in range(-3, NG + 3):
-            run(quantise_e, k - 2)
+            if k % 2 == 1 and 0 <= k - 3 < NG:
+                quantise_e((k - 3) // 2)
             run(group_e, k - 1)
             run(scores_matmul, k + 2)
-            run(values_matmul, k - 2)
-            run(normalise_and_store, k - 2)
+            run(values_matmul, k - 3)
+            run(normalise_and_store, k - 3)
             run(turn_queries, k + 3)
             if k == -1:
                 nc.scalar.copy(

@@ -47,17 +47,20 @@ def tile_mistralselfattention_pb_kernel(tc, q_rot, k_rot, v, mask_w, mask_b, out
         ps_out = ctx.enter_context(tc.psum_pool(name="ps_out", bufs=1))
         ctx.enter_context(tc.manual_schedule())
 
-        k_sb = keep.tile([P, QT, KV, D], BF16)
-        v_sb = keep.tile([P, 2, 2 * KV * D], BF16)
-        q_sb = [keep.tile([P, H, D], BF16, name="q_sb%d" % qt) for qt in range(QT)]
+        k_sb = [keep.tile([P, QT, D], BF16, name="k_sb%d" % kv) for kv in range(KV)]
+        q_sb = [keep.tile([P, G, D], BF16, name="q_sb%d" % g) for g in range(NG)]
         mw_sb = [keep.tile([P, T], BF16, name="mw_sb%d" % qt) for qt in range(QT)]
         mb_sb = [keep.tile([P, T], BF16, name="mb_sb%d" % qt) for qt in range(QT)]
-        nc.sync.dma_start(out=k_sb[:], in_=k_view)
-        for qt in range(QT):
-            nc.sync.dma_start(out=q_sb[qt][:], in_=q_view[:, qt])
-            nc.sync.dma_start(out=mw_sb[qt][:], in_=mw_view[:, qt])
-            nc.sync.dma_start(out=mb_sb[qt][:], in_=mb_view[:, qt])
+        v_sb = keep.tile([P, 2, 2 * KV * D], BF16)
+        for g in range(NG):
+            qt, kv = divmod(g, KV)
             if qt == 0:
+                nc.sync.dma_start(out=k_sb[kv][:], in_=k_view[:, :, kv, :])
+            nc.sync.dma_start(out=q_sb[g][:], in_=q_view[:, qt, kv * G : (kv + 1) * G, :])
+            if kv == 0:
+                nc.sync.dma_start(out=mw_sb[qt][:], in_=mw_view[:, qt])
+                nc.sync.dma_start(out=mb_sb[qt][:], in_=mb_view[:, qt])
+            if g == 1:
                 nc.sync.dma_start(out=v_sb[:], in_=v_view)
 
         ident_bf = keep.tile([P, P], BF16)
@@ -76,30 +79,33 @@ def tile_mistralselfattention_pb_kernel(tc, q_rot, k_rot, v, mask_w, mask_b, out
         tiles = {}
 
         def turn_queries(g):
-            qt, kv = divmod(g, KV)
             turned = ps_qk.tile([P, 2, G, P], BF16)
             for i in range(G):
-                nc.tensor.transpose(turned[:, 0, i, :], q_sb[qt][:, kv * G + i, :], ident_bf[:])
-            if qt == 0:
+                nc.tensor.transpose(turned[:, 0, i, :], q_sb[g][:, i, :], ident_bf[:])
+            if g < KV:
                 for kt in range(QT):
-                    nc.tensor.transpose(turned[:, 1, kt, :], k_sb[:, kt, kv, :], ident_bf[:])
-                nc.scalar.copy(out=kT[:, kv, :], in_=turned[:, 1].rearrange("d kt p -> d (kt p)"))
+                    nc.tensor.transpose(turned[:, 1, kt, :], k_sb[g][:, kt, :], ident_bf[:])
+            tiles["turned", g] = turned
+
+        def copy_queries(g):
+            turned = tiles["turned", g]
+            if g < KV:
+                nc.scalar.copy(out=kT[:, g, :], in_=turned[:, 1].rearrange("d kt p -> d (kt p)"))
             qT = work.tile([P, G, P], BF16)
             nc.scalar.copy(out=qT[:], in_=turned[:, 0])
             tiles["qT", g] = qT
 
         def scores_matmul(g):
-            kv = g % KV
             for i in range(G):
                 s_ps = ps_scores.tile([P, T], F32)
                 nc.tensor.matmul(
-                    s_ps[:], lhsT=tiles["qT", g][:, i, :], rhs=kT[:, kv, :], start=True, stop=True
+                    s_ps[:], lhsT=tiles["qT", g][:, i, :], rhs=kT[:, g % KV, :], start=True, stop=True
                 )
                 tiles["s_ps", g, i] = s_ps
 
         def weigh_scores(g):
             qt = g // KV
-            s2 = work.tile([P, G, T], F32)
+            s2 = work.tile([P, G, T], F32, bufs=4)
             for i in range(G):
                 nc.vector.scalar_tensor_tensor(
                     out=s2[:, i, :], in0=tiles["s_ps", g, i][:], scalar=SCALE, in1=mw_sb[qt][:],
@@ -114,23 +120,24 @@ def tile_mistralselfattention_pb_kernel(tc, q_rot, k_rot, v, mask_w, mask_b, out
 
         def row_maxima(g):
             neg_max = work.tile([P, G], F32)
-            nc.vector.tensor_reduce(
-                out=neg_max[:], in_=tiles["s2", g][:], axis=AXIS.X, op=ALU.max, negate=True
-            )
+            for i in range(G):
+                nc.vector.tensor_reduce(
+                    out=neg_max[:, i : i + 1], in_=tiles["s2", g][:, i, :], axis=AXIS.X, op=ALU.max,
+                    negate=True,
+                )
             tiles["neg_max", g] = neg_max
 
         def exponentials(g):
             e_sb = work.tile([P, G, T], BF16)
-            if g % 2 == 0:
-                tiles["rowsum", g // 2] = work.tile([P, 2, G], F32, name="rowsum")
-            rowsum = tiles["rowsum", g // 2]
+            rowsum = work.tile([P, G], F32, bufs=4)
             for i in range(G):
                 nc.scalar.activation(
                     out=e_sb[:, i, :], in_=tiles["s2", g][:, i, :], func=ACT.Exp,
                     bias=tiles["neg_max", g][:, i : i + 1], scale=1.0,
-                    accum_out=rowsum[:, g % 2, i : i + 1],
+                    accum_out=rowsum[:, i : i + 1],
                 )
             tiles["e_sb", g] = e_sb
+            tiles["rowsum", g] = rowsum
 
         def turn_e(g):
             for pair in range(G // 2):
@@ -144,36 +151,33 @@ def tile_mistralselfattention_pb_kernel(tc, q_rot, k_rot, v, mask_w, mask_b, out
                 tiles["eT_ps", g, pair] = eT_ps
 
         def group_e(g):
-            if g % 2 == 0:
-                tiles["e_grouped", g // 2] = work.tile(
-                    [P, 2, G, P, PACK], BF16, name="e_grouped", align_bytes=64
-                )
-            e_grouped = tiles["e_grouped", g // 2]
+            e_grouped = work.tile([P, G, P, PACK], BF16, align_bytes=64)
             for pair in range(G // 2):
                 nc.scalar.copy(
-                    out=e_grouped[:, g % 2, 2 * pair : 2 * pair + 2].bitcast(F32),
+                    out=e_grouped[:, 2 * pair : 2 * pair + 2].bitcast(F32),
                     in_=tiles["eT_ps", g, pair][:].rearrange("p j u q -> p j q u"),
                 )
+            tiles["e_grouped", g] = e_grouped
 
-        def quantise_e(two):
-            recip = work.tile([P, 2, G], F32)
-            nc.vector.reciprocal(out=recip[:], in_=tiles["rowsum", two][:])
-            tiles["recip", two] = recip
-            if two == 0:
+        def quantise_e(g):
+            recip = work.tile([P, G], F32)
+            nc.vector.reciprocal(out=recip[:], in_=tiles["rowsum", g][:])
+            tiles["recip", g] = recip
+            if g == 0:
                 nc.vector.quantize_mx(
                     out=v_codes[:].bitcast(FP8X4),
                     scales=v_scales[:],
                     in_=v_grouped[:].rearrange("p c t -> p (c t)"),
                 )
-            e_codes = work.tile([P, 2, G, P], U32, align_bytes=64)
-            e_scales = work.tile([P, 2, G, P], U8, align_bytes=64)
+            e_codes = work.tile([P, G * P], U32, align_bytes=64)
+            e_scales = work.tile([P, G * P], U8, align_bytes=64)
             nc.vector.quantize_mx(
-                out=e_codes[:].rearrange("p a i q -> p (a i q)").bitcast(FP8X4),
-                scales=e_scales[:].rearrange("p a i q -> p (a i q)"),
-                in_=tiles["e_grouped", two][:].rearrange("p a i q t -> p (a i q t)"),
+                out=e_codes[:].bitcast(FP8X4),
+                scales=e_scales[:],
+                in_=tiles["e_grouped", g][:].rearrange("p i q t -> p (i q t)"),
             )
-            tiles["e_codes", two] = e_codes
-            tiles["e_scales", two] = e_scales
+            tiles["e_codes", g] = e_codes
+            tiles["e_scales", g] = e_scales
 
         def values_matmul(g):
             kv = g % KV
@@ -181,8 +185,8 @@ def tile_mistralselfattention_pb_kernel(tc, q_rot, k_rot, v, mask_w, mask_b, out
             for i in range(G):
                 nc.tensor.matmul_mx(
                     out=o_ps[:, i, :],
-                    lhsT=tiles["e_codes", g // 2][:, g % 2, i, :].bitcast(FP8X4),
-                    lhsT_scale=tiles["e_scales", g // 2][:, g % 2, i, :],
+                    lhsT=tiles["e_codes", g][:, i * P : (i + 1) * P].bitcast(FP8X4),
+                    lhsT_scale=tiles["e_scales", g][:, i * P : (i + 1) * P],
                     rhs=v_codes[:, kv * D : (kv + 1) * D].bitcast(FP8X4),
                     rhs_scale=v_scales[:, kv * D : (kv + 1) * D],
                     start=True,
@@ -196,7 +200,7 @@ def tile_mistralselfattention_pb_kernel(tc, q_rot, k_rot, v, mask_w, mask_b, out
             for i in range(G):
                 nc.scalar.activation(
                     out=o_sb[:, i, :], in_=tiles["o_ps", g][:, i, :], func=ACT.Copy,
-                    scale=tiles["recip", g // 2][:, g % 2, i : i + 1],
+                    scale=tiles["recip", g][:, i : i + 1],
                 )
             nc.sync.dma_start(out=out_view[:, qt, kv * G : (kv + 1) * G, :], in_=o_sb[:])
 
@@ -204,19 +208,19 @@ def tile_mistralselfattention_pb_kernel(tc, q_rot, k_rot, v, mask_w, mask_b, out
             if 0 <= g < NG:
                 stage(g)
 
-        for k in range(-3, NG + 3):
-            if k % 2 == 1 and 0 <= k - 3 < NG:
-                quantise_e((k - 3) // 2)
-            run(group_e, k - 1)
-            run(scores_matmul, k + 2)
-            run(values_matmul, k - 3)
-            run(normalise_and_store, k - 3)
-            run(turn_queries, k + 3)
-            if k == -1:
-                nc.scalar.copy(
-                    out=v_grouped[:], in_=v_sb[:].rearrange("p u (e c) -> p c (u e)", e=2)
-                )
+        for k in range(-4, NG + 2):
+            run(quantise_e, k - 2)
+            run(scores_matmul, k + 3)
+            run(values_matmul, k - 2)
+            run(turn_queries, k + 4)
             run(row_maxima, k)
             run(exponentials, k)
             run(turn_e, k)
-            run(weigh_scores, k + 2)
+            run(normalise_and_store, k - 2)
+            run(copy_queries, k + 4)
+            if k == -2:
+                nc.scalar.copy(
+                    out=v_grouped[:], in_=v_sb[:].rearrange("p u (e c) -> p c (u e)", e=2)
+                )
+            run(group_e, k)
+            run(weigh_scores, k + 3)

@@ -23,6 +23,7 @@ QT = T // P
 PACK = 4
 HALF = T // 2
 NG = QT * KV
+HALVED = 1
 SCALE = 1.0 / math.sqrt(D)
 
 FLOPS = 2 * 2 * H * T * T * D
@@ -38,12 +39,19 @@ def tile_mistralselfattention_pb_kernel(tc, q_rot, k_rot, v, mask_w, mask_b, out
     out_view = out.rearrange("b (qt p) h d -> p (b qt) h d", p=P)
     v_view = v.rearrange("b (u p e) kv d -> p (b u) (e kv d)", u=2, p=P, e=2)
 
+    units = []
+    for g in range(NG):
+        heads = G // 2 if g >= NG - HALVED else G
+        for first in range(0, G, heads):
+            units.append((g // KV, g % KV, first, heads))
+    n_units = len(units)
+
     with ExitStack() as ctx:
         keep = ctx.enter_context(tc.tile_pool(name="keep", bufs=1))
         work = ctx.enter_context(tc.tile_pool(name="work", bufs=3))
         ps_scores = ctx.enter_context(tc.psum_pool(name="ps_scores", bufs=G))
         ps_e = ctx.enter_context(tc.psum_pool(name="ps_e", bufs=2))
-        ps_qk = ctx.enter_context(tc.psum_pool(name="ps_qk", bufs=1))
+        ps_q = ctx.enter_context(tc.psum_pool(name="ps_q", bufs=1))
         ps_out = ctx.enter_context(tc.psum_pool(name="ps_out", bufs=1))
         ctx.enter_context(tc.manual_schedule())
 
@@ -78,92 +86,99 @@ def tile_mistralselfattention_pb_kernel(tc, q_rot, k_rot, v, mask_w, mask_b, out
 
         tiles = {}
 
-        def turn_queries(g):
-            turned = ps_qk.tile([P, 2, G, P], BF16)
-            for i in range(G):
-                nc.tensor.transpose(turned[:, 0, i, :], q_sb[g][:, i, :], ident_bf[:])
-            if g < KV:
+        def turn_queries(u):
+            qt, kv, first, heads = units[u]
+            if qt == 0:
+                kT_ps = ps_e.tile([P, QT, P], BF16, tag="eT_ps")
                 for kt in range(QT):
-                    nc.tensor.transpose(turned[:, 1, kt, :], k_sb[g][:, kt, :], ident_bf[:])
-            tiles["turned", g] = turned
+                    nc.tensor.transpose(kT_ps[:, kt, :], k_sb[kv][:, kt, :], ident_bf[:])
+                tiles["kT_ps", u] = kT_ps
+            qT_ps = ps_q.tile([P, G, P], BF16)
+            for i in range(heads):
+                nc.tensor.transpose(qT_ps[:, i, :], q_sb[qt * KV + kv][:, first + i, :], ident_bf[:])
+            tiles["qT_ps", u] = qT_ps
 
-        def copy_queries(g):
-            turned = tiles["turned", g]
-            if g < KV:
-                nc.scalar.copy(out=kT[:, g, :], in_=turned[:, 1].rearrange("d kt p -> d (kt p)"))
+        def copy_queries(u):
+            qt, kv, first, heads = units[u]
+            if qt == 0:
+                nc.scalar.copy(
+                    out=kT[:, kv, :], in_=tiles["kT_ps", u][:].rearrange("d kt p -> d (kt p)")
+                )
             qT = work.tile([P, G, P], BF16)
-            nc.scalar.copy(out=qT[:], in_=turned[:, 0])
-            tiles["qT", g] = qT
+            nc.scalar.copy(out=qT[:, :heads], in_=tiles["qT_ps", u][:, :heads])
+            tiles["qT", u] = qT
 
-        def scores_matmul(g):
-            for i in range(G):
+        def scores_matmul(u):
+            qt, kv, first, heads = units[u]
+            for i in range(heads):
                 s_ps = ps_scores.tile([P, T], F32)
                 nc.tensor.matmul(
-                    s_ps[:], lhsT=tiles["qT", g][:, i, :], rhs=kT[:, g % KV, :], start=True, stop=True
+                    s_ps[:], lhsT=tiles["qT", u][:, i, :], rhs=kT[:, kv, :], start=True, stop=True
                 )
-                tiles["s_ps", g, i] = s_ps
+                tiles["s_ps", u, i] = s_ps
 
-        def weigh_scores(g):
-            qt = g // KV
+        def weigh_scores(u):
+            qt, kv, first, heads = units[u]
             s2 = work.tile([P, G, T], F32, bufs=4)
-            for i in range(G):
+            for i in range(heads):
                 nc.vector.scalar_tensor_tensor(
-                    out=s2[:, i, :], in0=tiles["s_ps", g, i][:], scalar=SCALE, in1=mw_sb[qt][:],
+                    out=s2[:, i, :], in0=tiles["s_ps", u, i][:], scalar=SCALE, in1=mw_sb[qt][:],
                     op0=ALU.mult, op1=ALU.mult,
                 )
             nc.gpsimd.tensor_tensor(
-                out=s2[:], in0=s2[:],
-                in1=mb_sb[qt][:].unsqueeze(1).to_broadcast([P, G, T]),
+                out=s2[:, :heads], in0=s2[:, :heads],
+                in1=mb_sb[qt][:].unsqueeze(1).to_broadcast([P, heads, T]),
                 op=ALU.add,
             )
-            tiles["s2", g] = s2
+            tiles["s2", u] = s2
 
-        def row_maxima(g):
+        def row_maxima(u):
             neg_max = work.tile([P, G], F32)
-            for i in range(G):
+            for i in range(units[u][3]):
                 nc.vector.tensor_reduce(
-                    out=neg_max[:, i : i + 1], in_=tiles["s2", g][:, i, :], axis=AXIS.X, op=ALU.max,
+                    out=neg_max[:, i : i + 1], in_=tiles["s2", u][:, i, :], axis=AXIS.X, op=ALU.max,
                     negate=True,
                 )
-            tiles["neg_max", g] = neg_max
+            tiles["neg_max", u] = neg_max
 
-        def exponentials(g):
+        def exponentials(u):
             e_sb = work.tile([P, G, T], BF16)
             rowsum = work.tile([P, G], F32, bufs=4)
-            for i in range(G):
+            for i in range(units[u][3]):
                 nc.scalar.activation(
-                    out=e_sb[:, i, :], in_=tiles["s2", g][:, i, :], func=ACT.Exp,
-                    bias=tiles["neg_max", g][:, i : i + 1], scale=1.0,
+                    out=e_sb[:, i, :], in_=tiles["s2", u][:, i, :], func=ACT.Exp,
+                    bias=tiles["neg_max", u][:, i : i + 1], scale=1.0,
                     accum_out=rowsum[:, i : i + 1],
                 )
-            tiles["e_sb", g] = e_sb
-            tiles["rowsum", g] = rowsum
+            tiles["e_sb", u] = e_sb
+            tiles["rowsum", u] = rowsum
 
-        def turn_e(g):
-            for pair in range(G // 2):
+        def turn_e(u):
+            for first in range(0, units[u][3], 2):
                 eT_ps = ps_e.tile([P, 2, 2, P], F32)
                 for j in range(2):
-                    e_words = tiles["e_sb", g][:, 2 * pair + j, :].bitcast(F32)
-                    for u in range(2):
+                    e_words = tiles["e_sb", u][:, first + j, :].bitcast(F32)
+                    for half in range(2):
                         nc.tensor.transpose(
-                            eT_ps[:, j, u, :], e_words[:, u * P : (u + 1) * P], ident_f32[:]
+                            eT_ps[:, j, half, :], e_words[:, half * P : (half + 1) * P], ident_f32[:]
                         )
-                tiles["eT_ps", g, pair] = eT_ps
+                tiles["eT_ps", u, first] = eT_ps
 
-        def group_e(g):
+        def group_e(u):
             e_grouped = work.tile([P, G, P, PACK], BF16, align_bytes=64)
-            for pair in range(G // 2):
+            for first in range(0, units[u][3], 2):
                 nc.scalar.copy(
-                    out=e_grouped[:, 2 * pair : 2 * pair + 2].bitcast(F32),
-                    in_=tiles["eT_ps", g, pair][:].rearrange("p j u q -> p j q u"),
+                    out=e_grouped[:, first : first + 2].bitcast(F32),
+                    in_=tiles["eT_ps", u, first][:].rearrange("p j half q -> p j q half"),
                 )
-            tiles["e_grouped", g] = e_grouped
+            tiles["e_grouped", u] = e_grouped
 
-        def quantise_e(g):
+        def quantise_e(u):
+            heads = units[u][3]
             recip = work.tile([P, G], F32)
-            nc.vector.reciprocal(out=recip[:], in_=tiles["rowsum", g][:])
-            tiles["recip", g] = recip
-            if g == 0:
+            nc.vector.reciprocal(out=recip[:, :heads], in_=tiles["rowsum", u][:, :heads])
+            tiles["recip", u] = recip
+            if u == 0:
                 nc.vector.quantize_mx(
                     out=v_codes[:].bitcast(FP8X4),
                     scales=v_scales[:],
@@ -172,43 +187,44 @@ def tile_mistralselfattention_pb_kernel(tc, q_rot, k_rot, v, mask_w, mask_b, out
             e_codes = work.tile([P, G * P], U32, align_bytes=64)
             e_scales = work.tile([P, G * P], U8, align_bytes=64)
             nc.vector.quantize_mx(
-                out=e_codes[:].bitcast(FP8X4),
-                scales=e_scales[:],
-                in_=tiles["e_grouped", g][:].rearrange("p i q t -> p (i q t)"),
+                out=e_codes[:, : heads * P].bitcast(FP8X4),
+                scales=e_scales[:, : heads * P],
+                in_=tiles["e_grouped", u][:, :heads].rearrange("p i q t -> p (i q t)"),
             )
-            tiles["e_codes", g] = e_codes
-            tiles["e_scales", g] = e_scales
+            tiles["e_codes", u] = e_codes
+            tiles["e_scales", u] = e_scales
 
-        def values_matmul(g):
-            kv = g % KV
+        def values_matmul(u):
+            qt, kv, first, heads = units[u]
             o_ps = ps_out.tile([P, G, D], F32)
-            for i in range(G):
+            for i in range(heads):
                 nc.tensor.matmul_mx(
                     out=o_ps[:, i, :],
-                    lhsT=tiles["e_codes", g][:, i * P : (i + 1) * P].bitcast(FP8X4),
-                    lhsT_scale=tiles["e_scales", g][:, i * P : (i + 1) * P],
+                    lhsT=tiles["e_codes", u][:, i * P : (i + 1) * P].bitcast(FP8X4),
+                    lhsT_scale=tiles["e_scales", u][:, i * P : (i + 1) * P],
                     rhs=v_codes[:, kv * D : (kv + 1) * D].bitcast(FP8X4),
                     rhs_scale=v_scales[:, kv * D : (kv + 1) * D],
                     start=True,
                     stop=True,
                 )
-            tiles["o_ps", g] = o_ps
+            tiles["o_ps", u] = o_ps
 
-        def normalise_and_store(g):
-            qt, kv = divmod(g, KV)
+        def normalise_and_store(u):
+            qt, kv, first, heads = units[u]
             o_sb = work.tile([P, G, D], F32)
-            for i in range(G):
+            for i in range(heads):
                 nc.scalar.activation(
-                    out=o_sb[:, i, :], in_=tiles["o_ps", g][:, i, :], func=ACT.Copy,
-                    scale=tiles["recip", g][:, i : i + 1],
+                    out=o_sb[:, i, :], in_=tiles["o_ps", u][:, i, :], func=ACT.Copy,
+                    scale=tiles["recip", u][:, i : i + 1],
                 )
-            nc.sync.dma_start(out=out_view[:, qt, kv * G : (kv + 1) * G, :], in_=o_sb[:])
+            h0 = kv * G + first
+            nc.sync.dma_start(out=out_view[:, qt, h0 : h0 + heads, :], in_=o_sb[:, :heads])
 
-        def run(stage, g):
-            if 0 <= g < NG:
-                stage(g)
+        def run(stage, u):
+            if 0 <= u < n_units:
+                stage(u)
 
-        for k in range(-4, NG + 2):
+        for k in range(-4, n_units + 2):
             run(quantise_e, k - 2)
             run(scores_matmul, k + 3)
             run(values_matmul, k - 2)

@@ -20,11 +20,15 @@ KV = 4
 D = 128
 G = H // KV
 QT = T // P
-PACK = 4
-HALF = T // 2
 NG = QT * KV
-HALVED = 1
+PACK = 4
 SCALE = 1.0 / math.sqrt(D)
+
+TURN_AHEAD = 4
+SCORES_AHEAD = 3
+VALUES_BEHIND = 2
+V_ROUND = -2
+HALVED = 1
 
 FLOPS = 2 * 2 * H * T * T * D
 
@@ -37,7 +41,7 @@ def tile_mistralselfattention_pb_kernel(tc, q_rot, k_rot, v, mask_w, mask_b, out
     mw_view = mask_w.rearrange("a b (qt p) k -> p (a b qt) k", p=P)
     mb_view = mask_b.rearrange("a b (qt p) k -> p (a b qt) k", p=P)
     out_view = out.rearrange("b (qt p) h d -> p (b qt) h d", p=P)
-    v_view = v.rearrange("b (u p e) kv d -> p (b u) (e kv d)", u=2, p=P, e=2)
+    v_view = v.rearrange("b (half p e) kv d -> p (b half) (e kv d)", half=2, p=P, e=2)
 
     units = []
     for g in range(NG):
@@ -68,7 +72,7 @@ def tile_mistralselfattention_pb_kernel(tc, q_rot, k_rot, v, mask_w, mask_b, out
             if kv == 0:
                 nc.sync.dma_start(out=mw_sb[qt][:], in_=mw_view[:, qt])
                 nc.sync.dma_start(out=mb_sb[qt][:], in_=mb_view[:, qt])
-            if g == 1:
+            if g == TURN_AHEAD + V_ROUND - 1:
                 nc.sync.dma_start(out=v_sb[:], in_=v_view)
 
         ident_bf = keep.tile([P, P], BF16)
@@ -119,7 +123,7 @@ def tile_mistralselfattention_pb_kernel(tc, q_rot, k_rot, v, mask_w, mask_b, out
 
         def weigh_scores(u):
             qt, kv, first, heads = units[u]
-            s2 = work.tile([P, G, T], F32, bufs=4)
+            s2 = work.tile([P, G, T], F32, bufs=SCORES_AHEAD + 1)
             for i in range(heads):
                 nc.vector.scalar_tensor_tensor(
                     out=s2[:, i, :], in0=tiles["s_ps", u, i][:], scalar=SCALE, in1=mw_sb[qt][:],
@@ -143,7 +147,7 @@ def tile_mistralselfattention_pb_kernel(tc, q_rot, k_rot, v, mask_w, mask_b, out
 
         def exponentials(u):
             e_sb = work.tile([P, G, T], BF16)
-            rowsum = work.tile([P, G], F32, bufs=4)
+            rowsum = work.tile([P, G], F32)
             for i in range(units[u][3]):
                 nc.scalar.activation(
                     out=e_sb[:, i, :], in_=tiles["s2", u][:, i, :], func=ACT.Exp,
@@ -154,22 +158,22 @@ def tile_mistralselfattention_pb_kernel(tc, q_rot, k_rot, v, mask_w, mask_b, out
             tiles["rowsum", u] = rowsum
 
         def turn_e(u):
-            for first in range(0, units[u][3], 2):
+            for j0 in range(0, units[u][3], 2):
                 eT_ps = ps_e.tile([P, 2, 2, P], F32)
                 for j in range(2):
-                    e_words = tiles["e_sb", u][:, first + j, :].bitcast(F32)
+                    e_words = tiles["e_sb", u][:, j0 + j, :].bitcast(F32)
                     for half in range(2):
                         nc.tensor.transpose(
                             eT_ps[:, j, half, :], e_words[:, half * P : (half + 1) * P], ident_f32[:]
                         )
-                tiles["eT_ps", u, first] = eT_ps
+                tiles["eT_ps", u, j0] = eT_ps
 
         def group_e(u):
             e_grouped = work.tile([P, G, P, PACK], BF16, align_bytes=64)
-            for first in range(0, units[u][3], 2):
+            for j0 in range(0, units[u][3], 2):
                 nc.scalar.copy(
-                    out=e_grouped[:, first : first + 2].bitcast(F32),
-                    in_=tiles["eT_ps", u, first][:].rearrange("p j half q -> p j q half"),
+                    out=e_grouped[:, j0 : j0 + 2].bitcast(F32),
+                    in_=tiles["eT_ps", u, j0][:].rearrange("p j half q -> p j q half"),
                 )
             tiles["e_grouped", u] = e_grouped
 
@@ -224,19 +228,19 @@ def tile_mistralselfattention_pb_kernel(tc, q_rot, k_rot, v, mask_w, mask_b, out
             if 0 <= u < n_units:
                 stage(u)
 
-        for k in range(-4, n_units + 2):
-            run(quantise_e, k - 2)
-            run(scores_matmul, k + 3)
-            run(values_matmul, k - 2)
-            run(turn_queries, k + 4)
+        for k in range(-TURN_AHEAD, n_units + VALUES_BEHIND):
+            run(quantise_e, k - VALUES_BEHIND)
+            run(scores_matmul, k + SCORES_AHEAD)
+            run(values_matmul, k - VALUES_BEHIND)
+            run(turn_queries, k + TURN_AHEAD)
             run(row_maxima, k)
             run(exponentials, k)
             run(turn_e, k)
-            run(normalise_and_store, k - 2)
-            run(copy_queries, k + 4)
-            if k == -2:
+            run(normalise_and_store, k - VALUES_BEHIND)
+            run(copy_queries, k + TURN_AHEAD)
+            if k == V_ROUND:
                 nc.scalar.copy(
-                    out=v_grouped[:], in_=v_sb[:].rearrange("p u (e c) -> p c (u e)", e=2)
+                    out=v_grouped[:], in_=v_sb[:].rearrange("p half (e c) -> p c (half e)", e=2)
                 )
             run(group_e, k)
-            run(weigh_scores, k + 3)
+            run(weigh_scores, k + SCORES_AHEAD)

from contextlib import ExitStack
import math

import concourse.mybir as mybir
from concourse.masks import make_identity

BF16 = mybir.dt.bfloat16
F32 = mybir.dt.float32
U32 = mybir.dt.uint32
U8 = mybir.dt.uint8
FP8X4 = mybir.dt.float8_e4m3fn_x4
ALU = mybir.AluOpType
ACT = mybir.ActivationFunctionType
AXIS = mybir.AxisListType

P = 128
T = 512
H = 16
KV = 4
D = 128
G = H // KV
QT = T // P
NG = QT * KV
PACK = 4
SCALE = 1.0 / math.sqrt(D)

TURN_AHEAD = 4
SCORES_AHEAD = 3
VALUES_BEHIND = 2
V_ROUND = -2
HALVED = 1

FLOPS = 2 * 2 * H * T * T * D


def tile_mistralselfattention_pb_kernel(tc, q_rot, k_rot, v, mask_w, mask_b, out):
    nc = tc.nc

    q_view = q_rot.rearrange("b (qt p) h d -> p (b qt) h d", p=P)
    k_view = k_rot.rearrange("b (kt p) kv d -> p (b kt) kv d", p=P)
    mw_view = mask_w.rearrange("a b (qt p) k -> p (a b qt) k", p=P)
    mb_view = mask_b.rearrange("a b (qt p) k -> p (a b qt) k", p=P)
    out_view = out.rearrange("b (qt p) h d -> p (b qt) h d", p=P)
    v_view = v.rearrange("b (half p e) kv d -> p (b half) (e kv d)", half=2, p=P, e=2)

    units = []
    for g in range(NG):
        heads = G // 2 if g >= NG - HALVED else G
        for first in range(0, G, heads):
            units.append((g // KV, g % KV, first, heads))
    n_units = len(units)

    with ExitStack() as ctx:
        keep = ctx.enter_context(tc.tile_pool(name="keep", bufs=1))
        work = ctx.enter_context(tc.tile_pool(name="work", bufs=3))
        ps_scores = ctx.enter_context(tc.psum_pool(name="ps_scores", bufs=G))
        ps_e = ctx.enter_context(tc.psum_pool(name="ps_e", bufs=2))
        ps_q = ctx.enter_context(tc.psum_pool(name="ps_q", bufs=1))
        ps_out = ctx.enter_context(tc.psum_pool(name="ps_out", bufs=1))
        ctx.enter_context(tc.manual_schedule())

        k_sb = [keep.tile([P, QT, D], BF16, name="k_sb%d" % kv) for kv in range(KV)]
        q_sb = [keep.tile([P, G, D], BF16, name="q_sb%d" % g) for g in range(NG)]
        mw_sb = [keep.tile([P, T], BF16, name="mw_sb%d" % qt) for qt in range(QT)]
        mb_sb = [keep.tile([P, T], BF16, name="mb_sb%d" % qt) for qt in range(QT)]
        v_sb = keep.tile([P, 2, 2 * KV * D], BF16)
        for g in range(NG):
            qt, kv = divmod(g, KV)
            if qt == 0:
                nc.sync.dma_start(out=k_sb[kv][:], in_=k_view[:, :, kv, :])
            nc.sync.dma_start(out=q_sb[g][:], in_=q_view[:, qt, kv * G : (kv + 1) * G, :])
            if kv == 0:
                nc.sync.dma_start(out=mw_sb[qt][:], in_=mw_view[:, qt])
                nc.sync.dma_start(out=mb_sb[qt][:], in_=mb_view[:, qt])
            if g == TURN_AHEAD + V_ROUND - 1:
                nc.sync.dma_start(out=v_sb[:], in_=v_view)

        ident_bf = keep.tile([P, P], BF16)
        make_identity(nc, ident_bf[:])
        ident_f32 = keep.tile([P, P], F32)
        make_identity(nc, ident_f32[:])
        warm = keep.tile([P, 1], F32)
        nc.vector.memset(warm[:], 0.0)
        nc.scalar.activation(out=warm[:], in_=warm[:], func=ACT.Exp)

        kT = keep.tile([P, KV, T], BF16)
        v_grouped = keep.tile([P, KV * D, PACK], BF16, align_bytes=64)
        v_codes = keep.tile([P, KV * D], U32, align_bytes=64)
        v_scales = keep.tile([P, KV * D], U8, align_bytes=64)

        tiles = {}

        def turn_queries(u):
            qt, kv, first, heads = units[u]
            if qt == 0:
                kT_ps = ps_e.tile([P, QT, P], BF16, tag="eT_ps")
                for kt in range(QT):
                    nc.tensor.transpose(kT_ps[:, kt, :], k_sb[kv][:, kt, :], ident_bf[:])
                tiles["kT_ps", u] = kT_ps
            qT_ps = ps_q.tile([P, G, P], BF16)
            for i in range(heads):
                nc.tensor.transpose(qT_ps[:, i, :], q_sb[qt * KV + kv][:, first + i, :], ident_bf[:])
            tiles["qT_ps", u] = qT_ps

        def copy_queries(u):
            qt, kv, first, heads = units[u]
            if qt == 0:
                nc.scalar.copy(
                    out=kT[:, kv, :], in_=tiles["kT_ps", u][:].rearrange("d kt p -> d (kt p)")
                )
            qT = work.tile([P, G, P], BF16)
            nc.scalar.copy(out=qT[:, :heads], in_=tiles["qT_ps", u][:, :heads])
            tiles["qT", u] = qT

        def scores_matmul(u):
            qt, kv, first, heads = units[u]
            for i in range(heads):
                s_ps = ps_scores.tile([P, T], F32)
                nc.tensor.matmul(
                    s_ps[:], lhsT=tiles["qT", u][:, i, :], rhs=kT[:, kv, :], start=True, stop=True
                )
                tiles["s_ps", u, i] = s_ps

        def weigh_scores(u):
            qt, kv, first, heads = units[u]
            s2 = work.tile([P, G, T], F32, bufs=SCORES_AHEAD + 1)
            for i in range(heads):
                nc.vector.scalar_tensor_tensor(
                    out=s2[:, i, :], in0=tiles["s_ps", u, i][:], scalar=SCALE, in1=mw_sb[qt][:],
                    op0=ALU.mult, op1=ALU.mult,
                )
            nc.gpsimd.tensor_tensor(
                out=s2[:, :heads], in0=s2[:, :heads],
                in1=mb_sb[qt][:].unsqueeze(1).to_broadcast([P, heads, T]),
                op=ALU.add,
            )
            tiles["s2", u] = s2

        def row_maxima(u):
            neg_max = work.tile([P, G], F32)
            for i in range(units[u][3]):
                nc.vector.tensor_reduce(
                    out=neg_max[:, i : i + 1], in_=tiles["s2", u][:, i, :], axis=AXIS.X, op=ALU.max,
                    negate=True,
                )
            tiles["neg_max", u] = neg_max

        def exponentials(u):
            e_sb = work.tile([P, G, T], BF16)
            rowsum = work.tile([P, G], F32)
            for i in range(units[u][3]):
                nc.scalar.activation(
                    out=e_sb[:, i, :], in_=tiles["s2", u][:, i, :], func=ACT.Exp,
                    bias=tiles["neg_max", u][:, i : i + 1], scale=1.0,
                    accum_out=rowsum[:, i : i + 1],
                )
            tiles["e_sb", u] = e_sb
            tiles["rowsum", u] = rowsum

        def turn_e(u):
            for j0 in range(0, units[u][3], 2):
                eT_ps = ps_e.tile([P, 2, 2, P], F32)
                for j in range(2):
                    e_words = tiles["e_sb", u][:, j0 + j, :].bitcast(F32)
                    for half in range(2):
                        nc.tensor.transpose(
                            eT_ps[:, j, half, :], e_words[:, half * P : (half + 1) * P], ident_f32[:]
                        )
                tiles["eT_ps", u, j0] = eT_ps

        def group_e(u):
            e_grouped = work.tile([P, G, P, PACK], BF16, align_bytes=64)
            for j0 in range(0, units[u][3], 2):
                nc.scalar.copy(
                    out=e_grouped[:, j0 : j0 + 2].bitcast(F32),
                    in_=tiles["eT_ps", u, j0][:].rearrange("p j half q -> p j q half"),
                )
            tiles["e_grouped", u] = e_grouped

        def quantise_e(u):
            heads = units[u][3]
            recip = work.tile([P, G], F32)
            nc.vector.reciprocal(out=recip[:, :heads], in_=tiles["rowsum", u][:, :heads])
            tiles["recip", u] = recip
            if u == 0:
                nc.vector.quantize_mx(
                    out=v_codes[:].bitcast(FP8X4),
                    scales=v_scales[:],
                    in_=v_grouped[:].rearrange("p c t -> p (c t)"),
                )
            e_codes = work.tile([P, G * P], U32, align_bytes=64)
            e_scales = work.tile([P, G * P], U8, align_bytes=64)
            nc.vector.quantize_mx(
                out=e_codes[:, : heads * P].bitcast(FP8X4),
                scales=e_scales[:, : heads * P],
                in_=tiles["e_grouped", u][:, :heads].rearrange("p i q t -> p (i q t)"),
            )
            tiles["e_codes", u] = e_codes
            tiles["e_scales", u] = e_scales

        def values_matmul(u):
            qt, kv, first, heads = units[u]
            o_ps = ps_out.tile([P, G, D], F32)
            for i in range(heads):
                nc.tensor.matmul_mx(
                    out=o_ps[:, i, :],
                    lhsT=tiles["e_codes", u][:, i * P : (i + 1) * P].bitcast(FP8X4),
                    lhsT_scale=tiles["e_scales", u][:, i * P : (i + 1) * P],
                    rhs=v_codes[:, kv * D : (kv + 1) * D].bitcast(FP8X4),
                    rhs_scale=v_scales[:, kv * D : (kv + 1) * D],
                    start=True,
                    stop=True,
                )
            tiles["o_ps", u] = o_ps

        def normalise_and_store(u):
            qt, kv, first, heads = units[u]
            o_sb = work.tile([P, G, D], F32)
            for i in range(heads):
                nc.scalar.activation(
                    out=o_sb[:, i, :], in_=tiles["o_ps", u][:, i, :], func=ACT.Copy,
                    scale=tiles["recip", u][:, i : i + 1],
                )
            h0 = kv * G + first
            nc.sync.dma_start(out=out_view[:, qt, h0 : h0 + heads, :], in_=o_sb[:, :heads])

        def run(stage, u):
            if 0 <= u < n_units:
                stage(u)

        for k in range(-TURN_AHEAD, n_units + VALUES_BEHIND):
            run(quantise_e, k - VALUES_BEHIND)
            run(scores_matmul, k + SCORES_AHEAD)
            run(values_matmul, k - VALUES_BEHIND)
            run(turn_queries, k + TURN_AHEAD)
            run(row_maxima, k)
            run(exponentials, k)
            run(turn_e, k)
            run(normalise_and_store, k - VALUES_BEHIND)
            run(copy_queries, k + TURN_AHEAD)
            if k == V_ROUND:
                nc.scalar.copy(
                    out=v_grouped[:], in_=v_sb[:].rearrange("p half (e c) -> p c (half e)", e=2)
                )
            run(group_e, k)
            run(weigh_scores, k + SCORES_AHEAD)
